import numpy as np
import ml_dtypes


def mxq(x, axis, fmt="e4m3"):
    dtype, down = {"e4m3": (ml_dtypes.float8_e4m3fn, 7), "e5m2": (ml_dtypes.float8_e5m2, 14)}[fmt]
    v = np.moveaxis(np.asarray(x, np.float32).astype(ml_dtypes.bfloat16).astype(np.float64), axis, -1)
    blocks = v.reshape(v.shape[:-1] + (-1, 32))
    amax = np.abs(blocks).max(-1, keepdims=True)
    byte = np.maximum(np.where(amax > 0, np.frexp(amax)[1] - 1 + 127, 0) - down, 1)
    scale = np.exp2(byte - 127.0)
    codes = (blocks / scale).astype(np.float32).astype(dtype).astype(np.float64)
    return np.moveaxis((codes * scale).reshape(v.shape), -1, axis)


WIDE = False


def mx_kscale(k):
    if not WIDE:
        return np.ones(k)
    levels = np.array([20, -20, 10, -10, 0])
    a = np.random.permutation(np.resize(levels, k // 512 * 4)).reshape(k // 512, 4)
    idx = np.arange(k)
    return np.exp2(a[idx // 512, idx % 128 // 32])


BF16 = ml_dtypes.bfloat16


def bf(x):
    return np.asarray(x, np.float32).astype(BF16)


def f64(x):
    return np.asarray(x).astype(np.float64)


B, T, HP, WP, NH, D, DFF = 8, 7, 3, 3, 16, 512, 2048
HW = HP * WP
N = 1 + HW * T


def setup_inputs():
    u = mx_kscale(D)
    c = np.random.standard_normal((B * T, 1 + HW, D)) * 1.5 / np.sqrt(1 + HW)
    c[:, 0, :] *= 5.0
    xr = np.random.standard_normal((B, N, D)) * 1.1
    w = np.random.standard_normal((D, D)) / np.sqrt(D) / u[None, :]
    b = 0.1 * np.random.standard_normal(D)
    g = np.random.standard_normal((B, N, D)) * np.exp2(np.random.randint(-12, 1, (B, N, 1))) * 16.0 * u
    return {"ctx_s": bf(c),
            "x_res": bf(xr),
            "s_out_w": bf(w),
            "s_out_b": bf(b),
            "grad_out": bf(g)}


def reference(ctx_s, x_res, s_out_w, s_out_b, grad_out):
    g2 = f64(grad_out).reshape(B * N, D)
    h = mxq(g2, 1, "e5m2") @ mxq(f64(s_out_w), 1, "e4m3").T
    h = h.reshape(B, N, D)
    cls = np.broadcast_to(h[:, :1, :] / T, (B, T, D)).reshape(B * T, 1, D)
    pat = h[:, 1:, :].reshape(B, HW, T, D).swapaxes(1, 2).reshape(B * T, HW, D)
    return np.concatenate([cls, pat], axis=1)

@@ -1,0 +1,164 @@
+from contextlib import ExitStack
+
+import concourse.mybir as mybir
+from concourse.masks import make_identity
+
+BF16 = mybir.dt.bfloat16
+F32 = mybir.dt.float32
+U32 = mybir.dt.uint32
+U8 = mybir.dt.uint8
+E5M2_X4 = mybir.dt.float8_e5m2_x4
+E4M3_X4 = mybir.dt.float8_e4m3fn_x4
+
+P = 128
+SAMPLES = 8
+FRAMES = 7
+POSITIONS = 10
+TOKENS = 64
+D = 512
+
+HALVES = 2
+PASSES = POSITIONS // HALVES
+USED = SAMPLES * FRAMES * HALVES
+TILE_SAMPLES = P // TOKENS
+ROW_TILES = D // P
+SLOTS = TILE_SAMPLES * FRAMES * HALVES
+FULL_PASSES = PASSES - 1
+FULL_SORTED = FULL_PASSES * SLOTS
+TILE_SEQUENCES = TILE_SAMPLES * FRAMES
+WORD_PLANES = 2
+BANK_WORDS = 512
+
+FLOPS = 2 * SAMPLES * TOKENS * D * D
+BYTES = 2 * (SAMPLES * TOKENS * D + D * D) + 4 * SAMPLES * FRAMES * POSITIONS * D
+
+
+def tile_timesformerlayer_pc_s_kernel(tc, ctx_s, x_res, s_out_w, s_out_b, grad_out, out):
+    nc = tc.nc
+    with ExitStack() as ctx:
+        consts = ctx.enter_context(tc.tile_pool(name="consts", bufs=1))
+        loaded = ctx.enter_context(tc.tile_pool(name="loaded", bufs=2 * ROW_TILES))
+        operands = ctx.enter_context(tc.tile_pool(name="operands", bufs=1))
+        results = ctx.enter_context(tc.tile_pool(name="results", bufs=PASSES))
+        flip_banks = ctx.enter_context(tc.psum_pool(name="flip_banks", bufs=4))
+        acc_banks = ctx.enter_context(tc.psum_pool(name="acc_banks", bufs=4))
+
+        grad_rows = grad_out.rearrange("b n k -> (b n) k")
+        grad_tiles = []
+        weight_tiles = []
+        for source, tiles in ((grad_rows, grad_tiles), (s_out_w, weight_tiles)):
+            for r in range(ROW_TILES):
+                rows = loaded.tile([P, D], BF16)
+                nc.sync.dma_start(out=rows[:], in_=source[r * P : (r + 1) * P, :])
+                tiles.append(rows)
+
+        ident = consts.tile([P, P], F32)
+        make_identity(nc, ident[:])
+        sorter = consts.tile([P, P], F32)
+        full = sorter[:, 0:FULL_SORTED].rearrange(
+            "k (i l t h) -> k i l t h", i=FULL_PASSES, l=TILE_SAMPLES, t=FRAMES, h=HALVES
+        )
+        token = ident[:].rearrange("k (l n) -> k l n", l=TILE_SAMPLES)
+        for h in range(HALVES):
+            first = FRAMES * (PASSES * h + 1) - (FRAMES - 1)
+            nc.vector.tensor_copy(
+                out=full[:, :, :, :, h],
+                in_=token[:, :, first : first + FULL_PASSES * FRAMES].rearrange("k l (i t) -> k i l t", t=FRAMES),
+            )
+        first = FRAMES * PASSES - (FRAMES - 1)
+        nc.vector.tensor_copy(
+            out=sorter[:, FULL_SORTED : FULL_SORTED + TILE_SEQUENCES].rearrange("k (l t) -> k l t", t=FRAMES),
+            in_=token[:, :, first : first + FRAMES],
+        )
+        nc.vector.tensor_copy(out=sorter[:, FULL_SORTED + TILE_SEQUENCES : P], in_=token[:, :, 0])
+
+        grad_grouped = operands.tile([P, PASSES * P * 4], BF16, align_bytes=64)
+        grad_codes = operands.tile([P, PASSES * P], U32, align_bytes=64)
+        grad_scales = operands.tile([P, PASSES * P], U8, align_bytes=64)
+        weight_grouped = operands.tile([P, D * 4], BF16, align_bytes=64)
+        weight_codes = operands.tile([P, D], U32, align_bytes=64)
+        weight_scales = operands.tile([P, D], U8, align_bytes=64)
+        grad_words = grad_grouped[:].bitcast(F32).rearrange(
+            "k (i q u) -> k i q u", i=PASSES, q=P, u=WORD_PLANES
+        )
+        weight_words = weight_grouped[:].bitcast(F32).rearrange("k (c u) -> k c u", u=WORD_PLANES)
+        nc.vector.memset(grad_grouped[:].bitcast(F32), 0.0)
+
+        for r in range(ROW_TILES):
+            words = grad_tiles[r][:].bitcast(F32)
+            flipped = flip_banks.tile([P, WORD_PLANES, BANK_WORDS // WORD_PLANES], F32)
+            for u in range(WORD_PLANES):
+                nc.tensor.transpose(flipped[:, u, 0:P], words[:, u * P : (u + 1) * P], sorter[:])
+            mine = grad_words[:, :, r * SLOTS : (r + 1) * SLOTS, :]
+            moves = (
+                (
+                    mine[:, 1:PASSES, :, :],
+                    flipped[:, :, 0:FULL_SORTED].rearrange("k u (i c) -> k i c u", i=FULL_PASSES),
+                ),
+                (
+                    mine[:, 0, 1:SLOTS:HALVES, :],
+                    flipped[:, :, FULL_SORTED : FULL_SORTED + TILE_SEQUENCES].rearrange("k u c -> k c u"),
+                ),
+                (
+                    mine[:, 0, 0 : SLOTS : FRAMES * HALVES, :],
+                    flipped[:, :, FULL_SORTED + TILE_SEQUENCES : P].rearrange("k u c -> k c u"),
+                ),
+            )
+            for target, sorted_words in moves:
+                if r % 2 == 0:
+                    nc.vector.tensor_copy(out=target, in_=sorted_words)
+                else:
+                    nc.scalar.copy(out=target, in_=sorted_words)
+        for i in range(PASSES):
+            nc.vector.quantize_mx(
+                out=grad_codes[:, i * P : (i + 1) * P].bitcast(E5M2_X4),
+                scales=grad_scales[:, i * P : (i + 1) * P],
+                in_=grad_grouped[:, i * P * 4 : (i + 1) * P * 4],
+            )
+
+        for r in range(ROW_TILES):
+            words = weight_tiles[r][:].bitcast(F32)
+            flipped = flip_banks.tile([P, WORD_PLANES, BANK_WORDS // WORD_PLANES], F32)
+            for u in range(WORD_PLANES):
+                nc.tensor.transpose(flipped[:, u, 0:P], words[:, u * P : (u + 1) * P], ident[:])
+            nc.scalar.copy(
+                out=weight_words[:, r * P : (r + 1) * P, :],
+                in_=flipped[:, :, 0:P].rearrange("k u c -> k c u"),
+            )
+            nc.vector.quantize_mx(
+                out=weight_codes[:, r * P : (r + 1) * P].bitcast(E4M3_X4),
+                scales=weight_scales[:, r * P : (r + 1) * P],
+                in_=weight_grouped[:, r * P * 4 : (r + 1) * P * 4],
+            )
+
+        out_rows = out.rearrange("j s d -> (j s) d").rearrange("(q i) d -> q i d", i=PASSES)
+        class_rows_of_out = out.rearrange("(b t) s d -> b t s d", t=FRAMES)[:, :, 0, :]
+        for i in range(PASSES):
+            acc = acc_banks.tile([P, D], F32)
+            nc.tensor.matmul_mx(
+                out=acc[:],
+                lhsT=grad_codes[:, i * P : (i + 1) * P].bitcast(E5M2_X4),
+                lhsT_scale=grad_scales[:, i * P : (i + 1) * P],
+                rhs=weight_codes[:].bitcast(E4M3_X4),
+                rhs_scale=weight_scales[:],
+                start=True,
+                stop=True,
+            )
+            result = results.tile([P, D], F32)
+            if i == 0:
+                nc.vector.tensor_copy(out=result[:], in_=acc[:])
+                nc.sync.dma_start(out=out[:, PASSES, :], in_=result[1:USED:HALVES, :])
+                class_result = results.tile([P, D], F32)
+                nc.vector.tensor_scalar_mul(out=class_result[:], in0=acc[:], scalar1=1.0 / FRAMES)
+                nc.sync.dma_start(
+                    out=class_rows_of_out,
+                    in_=class_result[0 : USED : FRAMES * HALVES, :]
+                    .unsqueeze(1)
+                    .to_broadcast([SAMPLES, FRAMES, D]),
+                )
+            elif i % 2 == 0:
+                nc.vector.tensor_copy(out=result[:], in_=acc[:])
+                nc.sync.dma_start(out=out_rows[:, i, :], in_=result[0:USED, :])
+            else:
+                nc.scalar.copy(out=result[:], in_=acc[:])
+                nc.scalar.dma_start(out=out_rows[:, i, :], in_=result[0:USED, :])

@@ -16,21 +16,33 @@ FRAMES = 7
 POSITIONS = 10
 TOKENS = 64
 D = 512
+SEQUENCES = SAMPLES * FRAMES
 
-HALVES = 2
-PASSES = POSITIONS // HALVES
-USED = SAMPLES * FRAMES * HALVES
-TILE_SAMPLES = P // TOKENS
 ROW_TILES = D // P
-SLOTS = TILE_SAMPLES * FRAMES * HALVES
-FULL_PASSES = PASSES - 1
-FULL_SORTED = FULL_PASSES * SLOTS
+TILE_SAMPLES = P // TOKENS
 TILE_SEQUENCES = TILE_SAMPLES * FRAMES
+GROUPS = 2
+GROUP_TILES = ROW_TILES // GROUPS
+PAIRS = 4
+PAIR_ROWS = 2
+HALF = POSITIONS // 2
+MIDDLE = HALF
+TILE_COLUMNS = TILE_SEQUENCES * PAIRS
+USED = GROUP_TILES * TILE_COLUMNS
+PAIRED = PAIR_ROWS * TILE_COLUMNS
+PASSES = GROUPS * PAIR_ROWS + 1
+REST = PASSES - 1
+CLASS_STEP = 4
+MIDDLE_FIRST = SAMPLES * CLASS_STEP
 WORD_PLANES = 2
 BANK_WORDS = 512
 
 FLOPS = 2 * SAMPLES * TOKENS * D * D
-BYTES = 2 * (SAMPLES * TOKENS * D + D * D) + 4 * SAMPLES * FRAMES * POSITIONS * D
+BYTES = 2 * (SAMPLES * TOKENS * D + D * D) + 4 * SEQUENCES * POSITIONS * D
+
+
+def first_token(position):
+    return FRAMES * position - (FRAMES - 1)
 
 
 def tile_timesformerlayer_pc_s_kernel(tc, ctx_s, x_res, s_out_w, s_out_b, grad_out, out):
@@ -39,14 +51,14 @@ def tile_timesformerlayer_pc_s_kernel(tc, ctx_s, x_res, s_out_w, s_out_b, grad_o
         consts = ctx.enter_context(tc.tile_pool(name="consts", bufs=1))
         loaded = ctx.enter_context(tc.tile_pool(name="loaded", bufs=2 * ROW_TILES))
         operands = ctx.enter_context(tc.tile_pool(name="operands", bufs=1))
-        results = ctx.enter_context(tc.tile_pool(name="results", bufs=PASSES))
+        results = ctx.enter_context(tc.tile_pool(name="results", bufs=GROUPS))
         flip_banks = ctx.enter_context(tc.psum_pool(name="flip_banks", bufs=4))
         acc_banks = ctx.enter_context(tc.psum_pool(name="acc_banks", bufs=4))
 
         grad_rows = grad_out.rearrange("b n k -> (b n) k")
-        grad_tiles = []
         weight_tiles = []
-        for source, tiles in ((grad_rows, grad_tiles), (s_out_w, weight_tiles)):
+        grad_tiles = []
+        for source, tiles in ((s_out_w, weight_tiles), (grad_rows, grad_tiles)):
             for r in range(ROW_TILES):
                 rows = loaded.tile([P, D], BF16)
                 nc.sync.dma_start(out=rows[:], in_=source[r * P : (r + 1) * P, :])
@@ -55,22 +67,27 @@ def tile_timesformerlayer_pc_s_kernel(tc, ctx_s, x_res, s_out_w, s_out_b, grad_o
         ident = consts.tile([P, P], F32)
         make_identity(nc, ident[:])
         sorter = consts.tile([P, P], F32)
-        full = sorter[:, 0:FULL_SORTED].rearrange(
-            "k (i l t h) -> k i l t h", i=FULL_PASSES, l=TILE_SAMPLES, t=FRAMES, h=HALVES
+        paired = sorter[:, 0:PAIRED].rearrange(
+            "k (x l t w) -> k x l t w", x=PAIR_ROWS, l=TILE_SAMPLES, t=FRAMES, w=PAIRS
         )
         token = ident[:].rearrange("k (l n) -> k l n", l=TILE_SAMPLES)
-        for h in range(HALVES):
-            first = FRAMES * (PASSES * h + 1) - (FRAMES - 1)
+        for w in range(PAIRS):
+            first = first_token(HALF * (w // 2) + PAIR_ROWS * (w % 2) + 1)
             nc.vector.tensor_copy(
-                out=full[:, :, :, :, h],
-                in_=token[:, :, first : first + FULL_PASSES * FRAMES].rearrange("k l (i t) -> k i l t", t=FRAMES),
+                out=paired[:, :, :, :, w],
+                in_=token[:, :, first : first + PAIR_ROWS * FRAMES].rearrange("k l (x t) -> k x l t", t=FRAMES),
             )
-        first = FRAMES * PASSES - (FRAMES - 1)
         nc.vector.tensor_copy(
-            out=sorter[:, FULL_SORTED : FULL_SORTED + TILE_SEQUENCES].rearrange("k (l t) -> k l t", t=FRAMES),
-            in_=token[:, :, first : first + FRAMES],
+            out=sorter[:, PAIRED : PAIRED + TILE_SEQUENCES].rearrange("k (l t) -> k l t", t=FRAMES),
+            in_=token[:, :, first_token(MIDDLE) : first_token(MIDDLE) + FRAMES],
         )
-        nc.vector.tensor_copy(out=sorter[:, FULL_SORTED + TILE_SEQUENCES : P], in_=token[:, :, 0])
+        nc.vector.tensor_copy(out=sorter[:, PAIRED + TILE_SEQUENCES : P], in_=token[:, :, 0])
+
+        rest_scale = consts.tile([P, 1], F32)
+        nc.vector.memset(rest_scale[:], 1.0)
+        nc.vector.tensor_scalar_mul(
+            out=rest_scale[0:MIDDLE_FIRST, :], in0=rest_scale[0:MIDDLE_FIRST, :], scalar1=1.0 / FRAMES
+        )
 
         grad_grouped = operands.tile([P, PASSES * P * 4], BF16, align_bytes=64)
         grad_codes = operands.tile([P, PASSES * P], U32, align_bytes=64)
@@ -84,36 +101,11 @@ def tile_timesformerlayer_pc_s_kernel(tc, ctx_s, x_res, s_out_w, s_out_b, grad_o
         weight_words = weight_grouped[:].bitcast(F32).rearrange("k (c u) -> k c u", u=WORD_PLANES)
         nc.vector.memset(grad_grouped[:].bitcast(F32), 0.0)
 
-        for r in range(ROW_TILES):
-            words = grad_tiles[r][:].bitcast(F32)
-            flipped = flip_banks.tile([P, WORD_PLANES, BANK_WORDS // WORD_PLANES], F32)
-            for u in range(WORD_PLANES):
-                nc.tensor.transpose(flipped[:, u, 0:P], words[:, u * P : (u + 1) * P], sorter[:])
-            mine = grad_words[:, :, r * SLOTS : (r + 1) * SLOTS, :]
-            moves = (
-                (
-                    mine[:, 1:PASSES, :, :],
-                    flipped[:, :, 0:FULL_SORTED].rearrange("k u (i c) -> k i c u", i=FULL_PASSES),
-                ),
-                (
-                    mine[:, 0, 1:SLOTS:HALVES, :],
-                    flipped[:, :, FULL_SORTED : FULL_SORTED + TILE_SEQUENCES].rearrange("k u c -> k c u"),
-                ),
-                (
-                    mine[:, 0, 0 : SLOTS : FRAMES * HALVES, :],
-                    flipped[:, :, FULL_SORTED + TILE_SEQUENCES : P].rearrange("k u c -> k c u"),
-                ),
-            )
-            for target, sorted_words in moves:
-                if r % 2 == 0:
-                    nc.vector.tensor_copy(out=target, in_=sorted_words)
-                else:
-                    nc.scalar.copy(out=target, in_=sorted_words)
-        for i in range(PASSES):
+        def quantise_grad(first_pass, passes):
             nc.vector.quantize_mx(
-                out=grad_codes[:, i * P : (i + 1) * P].bitcast(E5M2_X4),
-                scales=grad_scales[:, i * P : (i + 1) * P],
-                in_=grad_grouped[:, i * P * 4 : (i + 1) * P * 4],
+                out=grad_codes[:, first_pass * P : (first_pass + passes) * P].bitcast(E5M2_X4),
+                scales=grad_scales[:, first_pass * P : (first_pass + passes) * P],
+                in_=grad_grouped[:, first_pass * P * 4 : (first_pass + passes) * P * 4],
             )
 
         for r in range(ROW_TILES):
@@ -131,9 +123,37 @@ def tile_timesformerlayer_pc_s_kernel(tc, ctx_s, x_res, s_out_w, s_out_b, grad_o
                 in_=weight_grouped[:, r * P * 4 : (r + 1) * P * 4],
             )
 
-        out_rows = out.rearrange("j s d -> (j s) d").rearrange("(q i) d -> q i d", i=PASSES)
-        class_rows_of_out = out.rearrange("(b t) s d -> b t s d", t=FRAMES)[:, :, 0, :]
-        for i in range(PASSES):
+        for a in range(GROUPS):
+            for half in range(GROUP_TILES):
+                r = a * GROUP_TILES + half
+                words = grad_tiles[r][:].bitcast(F32)
+                flipped = flip_banks.tile([P, WORD_PLANES, BANK_WORDS // WORD_PLANES], F32)
+                for u in range(WORD_PLANES):
+                    nc.tensor.transpose(flipped[:, u, 0:P], words[:, u * P : (u + 1) * P], sorter[:])
+                target = grad_words[
+                    :, a * PAIR_ROWS : (a + 1) * PAIR_ROWS, half * TILE_COLUMNS : (half + 1) * TILE_COLUMNS, :
+                ]
+                sorted_words = flipped[:, :, 0:PAIRED].rearrange("k u (x c) -> k x c u", x=PAIR_ROWS)
+                if half == 0:
+                    nc.vector.tensor_copy(out=target, in_=sorted_words)
+                else:
+                    nc.scalar.copy(out=target, in_=sorted_words)
+                nc.scalar.copy(
+                    out=grad_words[
+                        :, REST, MIDDLE_FIRST + r * TILE_SEQUENCES : MIDDLE_FIRST + (r + 1) * TILE_SEQUENCES, :
+                    ],
+                    in_=flipped[:, :, PAIRED : PAIRED + TILE_SEQUENCES].rearrange("k u c -> k c u"),
+                )
+                nc.scalar.copy(
+                    out=grad_words[
+                        :, REST, r * TILE_SAMPLES * CLASS_STEP : (r + 1) * TILE_SAMPLES * CLASS_STEP : CLASS_STEP, :
+                    ],
+                    in_=flipped[:, :, PAIRED + TILE_SEQUENCES : P].rearrange("k u c -> k c u"),
+                )
+            quantise_grad(a * PAIR_ROWS, PAIR_ROWS)
+        quantise_grad(REST, 1)
+
+        def multiply(i):
             acc = acc_banks.tile([P, D], F32)
             nc.tensor.matmul_mx(
                 out=acc[:],
@@ -144,21 +164,22 @@ def tile_timesformerlayer_pc_s_kernel(tc, ctx_s, x_res, s_out_w, s_out_b, grad_o
                 start=True,
                 stop=True,
             )
-            result = results.tile([P, D], F32)
-            if i == 0:
-                nc.vector.tensor_copy(out=result[:], in_=acc[:])
-                nc.sync.dma_start(out=out[:, PASSES, :], in_=result[1:USED:HALVES, :])
-                class_result = results.tile([P, D], F32)
-                nc.vector.tensor_scalar_mul(out=class_result[:], in0=acc[:], scalar1=1.0 / FRAMES)
-                nc.sync.dma_start(
-                    out=class_rows_of_out,
-                    in_=class_result[0 : USED : FRAMES * HALVES, :]
-                    .unsqueeze(1)
-                    .to_broadcast([SAMPLES, FRAMES, D]),
-                )
-            elif i % 2 == 0:
-                nc.vector.tensor_copy(out=result[:], in_=acc[:])
-                nc.sync.dma_start(out=out_rows[:, i, :], in_=result[0:USED, :])
-            else:
-                nc.scalar.copy(out=result[:], in_=acc[:])
-                nc.scalar.dma_start(out=out_rows[:, i, :], in_=result[0:USED, :])
+            return acc
+
+        out_runs = out.rearrange("j s d -> (j s) d").rearrange("(m i) d -> m i d", i=HALF)
+        group_runs = USED // 2
+        for a in range(GROUPS):
+            pair_rows = results.tile([P, PAIR_ROWS, D], F32)
+            nc.vector.tensor_copy(out=pair_rows[:, 0, :], in_=multiply(a * PAIR_ROWS)[:])
+            nc.scalar.copy(out=pair_rows[:, 1, :], in_=multiply(a * PAIR_ROWS + 1)[:])
+            runs = out_runs[a * group_runs : (a + 1) * group_runs, :, :]
+            nc.sync.dma_start(out=runs[:, 1 : 1 + PAIR_ROWS, :], in_=pair_rows[0:USED:2, :, :])
+            nc.scalar.dma_start(out=runs[:, 1 + PAIR_ROWS : 1 + 2 * PAIR_ROWS, :], in_=pair_rows[1:USED:2, :, :])
+
+        rest_rows = results.tile([P, D], F32)
+        nc.vector.tensor_scalar_mul(out=rest_rows[:], in0=multiply(REST)[:], scalar1=rest_scale[:, 0:1])
+        nc.sync.dma_start(out=out[:, MIDDLE, :], in_=rest_rows[MIDDLE_FIRST : MIDDLE_FIRST + SEQUENCES, :])
+        nc.scalar.dma_start(
+            out=out.rearrange("(b t) s d -> b t s d", t=FRAMES)[:, :, 0, :],
+            in_=rest_rows[0:MIDDLE_FIRST:CLASS_STEP, :].unsqueeze(1).to_broadcast([SAMPLES, FRAMES, D]),
+        )

@@ -179,7 +179,7 @@ def tile_timesformerlayer_pc_s_kernel(tc, ctx_s, x_res, s_out_w, s_out_b, grad_o
         rest_rows = results.tile([P, D], F32)
         nc.vector.tensor_scalar_mul(out=rest_rows[:], in0=multiply(REST)[:], scalar1=rest_scale[:, 0:1])
         nc.sync.dma_start(out=out[:, MIDDLE, :], in_=rest_rows[MIDDLE_FIRST : MIDDLE_FIRST + SEQUENCES, :])
-        nc.scalar.dma_start(
+        nc.sync.dma_start(
             out=out.rearrange("(b t) s d -> b t s d", t=FRAMES)[:, :, 0, :],
             in_=rest_rows[0:MIDDLE_FIRST:CLASS_STEP, :].unsqueeze(1).to_broadcast([SAMPLES, FRAMES, D]),
         )

from contextlib import ExitStack

import concourse.mybir as mybir
from concourse.masks import make_identity

BF16 = mybir.dt.bfloat16
F32 = mybir.dt.float32
U32 = mybir.dt.uint32
U8 = mybir.dt.uint8
E5M2_X4 = mybir.dt.float8_e5m2_x4
E4M3_X4 = mybir.dt.float8_e4m3fn_x4

P = 128
SAMPLES = 8
FRAMES = 7
POSITIONS = 10
TOKENS = 64
D = 512
SEQUENCES = SAMPLES * FRAMES

ROW_TILES = D // P
TILE_SAMPLES = P // TOKENS
TILE_SEQUENCES = TILE_SAMPLES * FRAMES
GROUPS = 2
GROUP_TILES = ROW_TILES // GROUPS
PAIRS = 4
PAIR_ROWS = 2
HALF = POSITIONS // 2
MIDDLE = HALF
TILE_COLUMNS = TILE_SEQUENCES * PAIRS
USED = GROUP_TILES * TILE_COLUMNS
PAIRED = PAIR_ROWS * TILE_COLUMNS
PASSES = GROUPS * PAIR_ROWS + 1
REST = PASSES - 1
CLASS_STEP = 4
MIDDLE_FIRST = SAMPLES * CLASS_STEP
WORD_PLANES = 2
BANK_WORDS = 512

FLOPS = 2 * SAMPLES * TOKENS * D * D
BYTES = 2 * (SAMPLES * TOKENS * D + D * D) + 4 * SEQUENCES * POSITIONS * D


def first_token(position):
    return FRAMES * position - (FRAMES - 1)


def tile_timesformerlayer_pc_s_kernel(tc, ctx_s, x_res, s_out_w, s_out_b, grad_out, out):
    nc = tc.nc
    with ExitStack() as ctx:
        consts = ctx.enter_context(tc.tile_pool(name="consts", bufs=1))
        loaded = ctx.enter_context(tc.tile_pool(name="loaded", bufs=2 * ROW_TILES))
        operands = ctx.enter_context(tc.tile_pool(name="operands", bufs=1))
        results = ctx.enter_context(tc.tile_pool(name="results", bufs=GROUPS))
        flip_banks = ctx.enter_context(tc.psum_pool(name="flip_banks", bufs=4))
        acc_banks = ctx.enter_context(tc.psum_pool(name="acc_banks", bufs=4))

        grad_rows = grad_out.rearrange("b n k -> (b n) k")
        weight_tiles = []
        grad_tiles = []
        for source, tiles in ((s_out_w, weight_tiles), (grad_rows, grad_tiles)):
            for r in range(ROW_TILES):
                rows = loaded.tile([P, D], BF16)
                nc.sync.dma_start(out=rows[:], in_=source[r * P : (r + 1) * P, :])
                tiles.append(rows)

        ident = consts.tile([P, P], F32)
        make_identity(nc, ident[:])
        sorter = consts.tile([P, P], F32)
        paired = sorter[:, 0:PAIRED].rearrange(
            "k (x l t w) -> k x l t w", x=PAIR_ROWS, l=TILE_SAMPLES, t=FRAMES, w=PAIRS
        )
        token = ident[:].rearrange("k (l n) -> k l n", l=TILE_SAMPLES)
        for w in range(PAIRS):
            first = first_token(HALF * (w // 2) + PAIR_ROWS * (w % 2) + 1)
            nc.vector.tensor_copy(
                out=paired[:, :, :, :, w],
                in_=token[:, :, first : first + PAIR_ROWS * FRAMES].rearrange("k l (x t) -> k x l t", t=FRAMES),
            )
        nc.vector.tensor_copy(
            out=sorter[:, PAIRED : PAIRED + TILE_SEQUENCES].rearrange("k (l t) -> k l t", t=FRAMES),
            in_=token[:, :, first_token(MIDDLE) : first_token(MIDDLE) + FRAMES],
        )
        nc.vector.tensor_copy(out=sorter[:, PAIRED + TILE_SEQUENCES : P], in_=token[:, :, 0])

        rest_scale = consts.tile([P, 1], F32)
        nc.vector.memset(rest_scale[:], 1.0)
        nc.vector.tensor_scalar_mul(
            out=rest_scale[0:MIDDLE_FIRST, :], in0=rest_scale[0:MIDDLE_FIRST, :], scalar1=1.0 / FRAMES
        )

        grad_grouped = operands.tile([P, PASSES * P * 4], BF16, align_bytes=64)
        grad_codes = operands.tile([P, PASSES * P], U32, align_bytes=64)
        grad_scales = operands.tile([P, PASSES * P], U8, align_bytes=64)
        weight_grouped = operands.tile([P, D * 4], BF16, align_bytes=64)
        weight_codes = operands.tile([P, D], U32, align_bytes=64)
        weight_scales = operands.tile([P, D], U8, align_bytes=64)
        grad_words = grad_grouped[:].bitcast(F32).rearrange(
            "k (i q u) -> k i q u", i=PASSES, q=P, u=WORD_PLANES
        )
        weight_words = weight_grouped[:].bitcast(F32).rearrange("k (c u) -> k c u", u=WORD_PLANES)
        nc.vector.memset(grad_grouped[:].bitcast(F32), 0.0)

        def quantise_grad(first_pass, passes):
            nc.vector.quantize_mx(
                out=grad_codes[:, first_pass * P : (first_pass + passes) * P].bitcast(E5M2_X4),
                scales=grad_scales[:, first_pass * P : (first_pass + passes) * P],
                in_=grad_grouped[:, first_pass * P * 4 : (first_pass + passes) * P * 4],
            )

        for r in range(ROW_TILES):
            words = weight_tiles[r][:].bitcast(F32)
            flipped = flip_banks.tile([P, WORD_PLANES, BANK_WORDS // WORD_PLANES], F32)
            for u in range(WORD_PLANES):
                nc.tensor.transpose(flipped[:, u, 0:P], words[:, u * P : (u + 1) * P], ident[:])
            nc.scalar.copy(
                out=weight_words[:, r * P : (r + 1) * P, :],
                in_=flipped[:, :, 0:P].rearrange("k u c -> k c u"),
            )
            nc.vector.quantize_mx(
                out=weight_codes[:, r * P : (r + 1) * P].bitcast(E4M3_X4),
                scales=weight_scales[:, r * P : (r + 1) * P],
                in_=weight_grouped[:, r * P * 4 : (r + 1) * P * 4],
            )

        for a in range(GROUPS):
            for half in range(GROUP_TILES):
                r = a * GROUP_TILES + half
                words = grad_tiles[r][:].bitcast(F32)
                flipped = flip_banks.tile([P, WORD_PLANES, BANK_WORDS // WORD_PLANES], F32)
                for u in range(WORD_PLANES):
                    nc.tensor.transpose(flipped[:, u, 0:P], words[:, u * P : (u + 1) * P], sorter[:])
                target = grad_words[
                    :, a * PAIR_ROWS : (a + 1) * PAIR_ROWS, half * TILE_COLUMNS : (half + 1) * TILE_COLUMNS, :
                ]
                sorted_words = flipped[:, :, 0:PAIRED].rearrange("k u (x c) -> k x c u", x=PAIR_ROWS)
                if half == 0:
                    nc.vector.tensor_copy(out=target, in_=sorted_words)
                else:
                    nc.scalar.copy(out=target, in_=sorted_words)
                nc.scalar.copy(
                    out=grad_words[
                        :, REST, MIDDLE_FIRST + r * TILE_SEQUENCES : MIDDLE_FIRST + (r + 1) * TILE_SEQUENCES, :
                    ],
                    in_=flipped[:, :, PAIRED : PAIRED + TILE_SEQUENCES].rearrange("k u c -> k c u"),
                )
                nc.scalar.copy(
                    out=grad_words[
                        :, REST, r * TILE_SAMPLES * CLASS_STEP : (r + 1) * TILE_SAMPLES * CLASS_STEP : CLASS_STEP, :
                    ],
                    in_=flipped[:, :, PAIRED + TILE_SEQUENCES : P].rearrange("k u c -> k c u"),
                )
            quantise_grad(a * PAIR_ROWS, PAIR_ROWS)
        quantise_grad(REST, 1)

        def multiply(i):
            acc = acc_banks.tile([P, D], F32)
            nc.tensor.matmul_mx(
                out=acc[:],
                lhsT=grad_codes[:, i * P : (i + 1) * P].bitcast(E5M2_X4),
                lhsT_scale=grad_scales[:, i * P : (i + 1) * P],
                rhs=weight_codes[:].bitcast(E4M3_X4),
                rhs_scale=weight_scales[:],
                start=True,
                stop=True,
            )
            return acc

        out_runs = out.rearrange("j s d -> (j s) d").rearrange("(m i) d -> m i d", i=HALF)
        group_runs = USED // 2
        for a in range(GROUPS):
            pair_rows = results.tile([P, PAIR_ROWS, D], F32)
            nc.vector.tensor_copy(out=pair_rows[:, 0, :], in_=multiply(a * PAIR_ROWS)[:])
            nc.scalar.copy(out=pair_rows[:, 1, :], in_=multiply(a * PAIR_ROWS + 1)[:])
            runs = out_runs[a * group_runs : (a + 1) * group_runs, :, :]
            nc.sync.dma_start(out=runs[:, 1 : 1 + PAIR_ROWS, :], in_=pair_rows[0:USED:2, :, :])
            nc.scalar.dma_start(out=runs[:, 1 + PAIR_ROWS : 1 + 2 * PAIR_ROWS, :], in_=pair_rows[1:USED:2, :, :])

        rest_rows = results.tile([P, D], F32)
        nc.vector.tensor_scalar_mul(out=rest_rows[:], in0=multiply(REST)[:], scalar1=rest_scale[:, 0:1])
        nc.sync.dma_start(out=out[:, MIDDLE, :], in_=rest_rows[MIDDLE_FIRST : MIDDLE_FIRST + SEQUENCES, :])
        nc.sync.dma_start(
            out=out.rearrange("(b t) s d -> b t s d", t=FRAMES)[:, :, 0, :],
            in_=rest_rows[0:MIDDLE_FIRST:CLASS_STEP, :].unsqueeze(1).to_broadcast([SAMPLES, FRAMES, D]),
        )
